import numpy as np
import ml_dtypes

BF16 = ml_dtypes.bfloat16


def bf(x):
    return np.asarray(x, np.float32).astype(BF16)


def f32(x):
    return np.asarray(x, np.float32)


def f64(x):
    return np.asarray(x).astype(np.float64)


def striped(idx):
    return np.tile(idx.reshape(-1, 16).T, (8, 1))


D, P, M, K, S, N = 512, 1024, 128, 4, 4096, 2048
EPS = 1e-5


def gelu_tanh(v):
    return 0.5 * v * (1.0 + np.tanh(np.sqrt(2.0 / np.pi) * (v + 0.044715 * v**3)))


def layer_norm(v, gain, shift):
    mu = v.mean(axis=0, keepdims=True)
    var = ((v - mu) ** 2).mean(axis=0, keepdims=True)
    return (v - mu) / np.sqrt(var + EPS) * gain + shift


def setup_inputs():
    return {
        "nodes": f32(np.random.standard_normal((D, K, N))),
        "meta": bf(np.random.standard_normal((M, N))),
        "w1": bf(np.random.standard_normal((P, D)) / np.sqrt(P)),
        "b1": f32(0.1 * np.random.standard_normal((D, 1))),
        "gain1": f32(1.0 + 0.1 * np.random.standard_normal((D, 1))),
        "shift1": f32(0.1 * np.random.standard_normal((D, 1))),
        "w2": bf(np.random.standard_normal((D, D)) / np.sqrt(D)),
        "b2": f32(0.1 * np.random.standard_normal((D, 1))),
        "v1": bf(np.random.standard_normal((M, D)) / np.sqrt(M)),
        "c1": f32(0.1 * np.random.standard_normal((D, 1))),
        "gain2": f32(1.0 + 0.1 * np.random.standard_normal((D, 1))),
        "shift2": f32(0.1 * np.random.standard_normal((D, 1))),
        "v2": bf(np.random.standard_normal((D, D)) / np.sqrt(D)),
        "c2": f32(0.1 * np.random.standard_normal((D, 1))),
        "base": f32(np.random.standard_normal((D, S))),
        "offs": striped(np.random.permutation(S)[:N]),
    }


def reference(nodes, meta, w1, b1, gain1, shift1, w2, b2, v1, c1, gain2, shift2, v2, c2, base, offs):
    idx = offs[:16].T.reshape(-1)
    nd = f64(nodes)
    pooled = np.concatenate([nd.sum(axis=1), nd.max(axis=1)], axis=0)
    u = f64(w1).T @ pooled + f64(b1)
    esub = f64(w2).T @ gelu_tanh(layer_norm(u, f64(gain1), f64(shift1))) + f64(b2)
    t = f64(v1).T @ f64(meta) + f64(c1)
    emeta = f64(v2).T @ gelu_tanh(layer_norm(t, f64(gain2), f64(shift2))) + f64(c2)
    out = f64(base).copy()
    out[:, idx] = esub + emeta
    return out

@@ -1,0 +1,176 @@
+import concourse.masks as masks
+import concourse.mybir as mybir
+
+F32 = mybir.dt.float32
+BF16 = mybir.dt.bfloat16
+U16 = mybir.dt.uint16
+ALU = mybir.AluOpType
+ACT = mybir.ActivationFunctionType
+
+P = 128
+D = 512
+NODES = 4
+N = 2048
+SLOTS = 4096
+EPS = 1e-5
+
+CHUNK = 512
+N_CHUNKS = N // CHUNK
+BLOCKS = D // P
+SUBS = CHUNK // P
+
+FLOPS = 2 * N * (2 * D * D + D * D + P * D + D * D)
+
+
+def tile_sgencoder_b_kernel(
+    tc, nodes, meta, w1, b1, gain1, shift1, w2, b2, v1, c1, gain2, shift2, v2, c2, base, offs, out
+):
+    nc = tc.nc
+    with (
+        tc.tile_pool(name="held", bufs=1) as held,
+        tc.tile_pool(name="work", bufs=2) as work,
+        tc.psum_pool(name="psum", bufs=2) as psum,
+    ):
+        offsets = held.tile([P, N // 16], U16, name="offsets")
+        nc.sync.dma_start(offsets[:], offs)
+
+        meta_sb = held.tile([P, N], BF16, name="meta_sb")
+        nc.scalar.dma_start(meta_sb[:], meta)
+        v1_sb = held.tile([P, D], BF16, name="v1_sb")
+        nc.scalar.dma_start(v1_sb[:], v1)
+        c1_rows = held.tile([P, D], F32, name="c1_rows")
+        nc.scalar.dma_start(c1_rows[:], c1.rearrange("h o -> (h o)").partition_broadcast(P))
+        b1_rows = held.tile([P, D], F32, name="b1_rows")
+        nc.scalar.dma_start(b1_rows[:], b1.rearrange("h o -> (h o)").partition_broadcast(P))
+
+        ident = held.tile([P, P], F32, name="ident")
+        masks.make_identity(nc, ident[:])
+        rows = held.tile([P, P], F32, name="rows")
+        nc.vector.memset(rows[:], 0.0)
+        for v, vector in enumerate((gain1, shift1, gain2, shift2, b2, c2)):
+            nc.scalar.dma_start(
+                rows[v * BLOCKS : (v + 1) * BLOCKS, :], vector.rearrange("(b p) o -> b (p o)", p=P)
+            )
+        cols_ps = psum.tile([P, CHUNK], F32, name="cols_ps", tag="turned", bufs=4)
+        nc.tensor.transpose(cols_ps[:, 0:P], rows[:], ident[:])
+        cols = held.tile([P, P], F32, name="cols")
+        nc.vector.tensor_copy(cols[:], cols_ps[:, 0:P])
+
+        def column(v, b):
+            return cols[:, v * BLOCKS + b : v * BLOCKS + b + 1]
+
+        w1_sb = held.tile([P, 2 * BLOCKS, D], BF16, name="w1_sb")
+        nc.scalar.dma_start(w1_sb[:], w1.rearrange("(b p) h -> p b h", p=P))
+        w2_sb = held.tile([P, BLOCKS, D], BF16, name="w2_sb")
+        nc.scalar.dma_start(w2_sb[:], w2.rearrange("(b p) c -> p b c", p=P))
+        v2_sb = held.tile([P, BLOCKS, D], BF16, name="v2_sb")
+        nc.scalar.dma_start(v2_sb[:], v2.rearrange("(b p) c -> p b c", p=P))
+
+        neg_half = held.tile([P, SUBS], F32, name="neg_half")
+        nc.vector.memset(neg_half[:], -0.5)
+
+        g1 = [held.tile([P, N], BF16, name=f"g1_{b}") for b in range(BLOCKS)]
+        g2 = [held.tile([P, N], BF16, name=f"g2_{b}") for b in range(BLOCKS)]
+
+        def pool_nodes(q):
+            pooled = work.tile([P, 2 * BLOCKS, CHUNK], BF16, name="pooled")
+            for b in range(BLOCKS):
+                nodes_sb = work.tile([P, NODES, CHUNK], F32, name="nodes_sb", bufs=4)
+                nc.sync.dma_start(
+                    nodes_sb[:], nodes[b * P : (b + 1) * P, :, q * CHUNK : (q + 1) * CHUNK]
+                )
+                pair_sum = work.tile([P, 2, CHUNK], F32, name="pair_sum")
+                nc.gpsimd.tensor_tensor(pair_sum[:], nodes_sb[:, 0:2, :], nodes_sb[:, 2:4, :], ALU.add)
+                nc.gpsimd.tensor_tensor(pooled[:, b, :], pair_sum[:, 0, :], pair_sum[:, 1, :], ALU.add)
+                pair_max = work.tile([P, 2, CHUNK], F32, name="pair_max")
+                nc.vector.tensor_tensor(pair_max[:], nodes_sb[:, 0:2, :], nodes_sb[:, 2:4, :], ALU.max)
+                nc.vector.tensor_tensor(
+                    pooled[:, BLOCKS + b, :], pair_max[:, 0, :], pair_max[:, 1, :], ALU.max
+                )
+            return pooled
+
+        def hidden_layer(q, terms, bias_rows, gain, shift, g):
+            total = work.tile([P, SUBS], F32, name="total", bufs=4)
+            u = [work.tile([P, D], F32, name="u", bufs=2 * SUBS) for s in range(SUBS)]
+            for s in range(SUBS):
+                u_ps = psum.tile([P, D], F32, name="u_ps")
+                for i, (inputs, weights) in enumerate(terms):
+                    nc.tensor.matmul(
+                        u_ps[:],
+                        inputs[:, s * P : (s + 1) * P],
+                        weights,
+                        start=(i == 0),
+                        stop=(i == len(terms) - 1),
+                    )
+                nc.vector.scalar_tensor_tensor(
+                    u[s][:], u_ps[:], 1.0, bias_rows[:], ALU.mult, ALU.add, accum_out=total[:, s : s + 1]
+                )
+            neg_mean = work.tile([P, SUBS], F32, name="neg_mean", bufs=4)
+            nc.vector.tensor_scalar_mul(neg_mean[:], total[:], -1.0 / D)
+
+            sq_total = work.tile([P, SUBS], F32, name="sq_total", bufs=4)
+            for s in range(SUBS):
+                squares = work.tile([P, D], BF16, name="squares")
+                nc.scalar.activation(
+                    squares[:],
+                    u[s][:],
+                    ACT.Square,
+                    bias=neg_mean[:, s : s + 1],
+                    accum_out=sq_total[:, s : s + 1],
+                )
+            var_eps = work.tile([P, SUBS], F32, name="var_eps", bufs=4)
+            nc.gpsimd.tensor_scalar(var_eps[:], sq_total[:], 1.0 / D, EPS, ALU.mult, ALU.add)
+            rstd = work.tile([P, SUBS], F32, name="rstd", bufs=4)
+            nc.gpsimd.tensor_tensor(rstd[:], var_eps[:], neg_half[:], ALU.pow)
+
+            normed = [work.tile([P, D], F32, name="normed", bufs=2 * SUBS) for s in range(SUBS)]
+            for s in range(SUBS):
+                nc.vector.tensor_scalar(
+                    normed[s][:], u[s][:], neg_mean[:, s : s + 1], rstd[:, s : s + 1], ALU.add, ALU.mult
+                )
+
+            for b in range(BLOCKS):
+                turned = psum.tile([P, CHUNK], F32, name="turned", bufs=4)
+                for s in range(SUBS):
+                    nc.tensor.transpose(
+                        turned[:, s * P : (s + 1) * P], normed[s][:, b * P : (b + 1) * P], ident[:]
+                    )
+                nc.scalar.activation(
+                    g[b][:, q * CHUNK : (q + 1) * CHUNK],
+                    turned[:],
+                    ACT.Gelu_apprx_tanh,
+                    bias=column(shift, b),
+                    scale=column(gain, b),
+                )
+
+        def output_layer(c, g, weights, bias, result):
+            for q in range(N_CHUNKS):
+                o_ps = psum.tile([P, CHUNK], F32, name="o_ps")
+                for b in range(BLOCKS):
+                    nc.tensor.matmul(
+                        o_ps[:],
+                        weights[:, b, c * P : (c + 1) * P],
+                        g[b][:, q * CHUNK : (q + 1) * CHUNK],
+                        start=(b == 0),
+                        stop=(b == BLOCKS - 1),
+                    )
+                nc.scalar.activation(
+                    result[:, q * CHUNK : (q + 1) * CHUNK], o_ps[:], ACT.Identity, bias=column(bias, c)
+                )
+
+        for q in range(N_CHUNKS):
+            pooled = pool_nodes(q)
+            hidden_layer(q, [(meta_sb[:, q * CHUNK : (q + 1) * CHUNK], v1_sb[:])], c1_rows, 2, 3, g2)
+            hidden_layer(
+                q, [(pooled[:, i, :], w1_sb[:, i, :]) for i in range(2 * BLOCKS)], b1_rows, 0, 1, g1
+            )
+
+        for c in range(BLOCKS):
+            esub = work.tile([P, N], F32, name="esub")
+            output_layer(c, g1, w2_sb, 4, esub)
+            emeta = work.tile([P, N], F32, name="emeta")
+            output_layer(c, g2, v2_sb, 5, emeta)
+            window = work.tile([P, SLOTS], F32, name="window")
+            nc.sync.dma_start(window[:], base[c * P : (c + 1) * P, :])
+            nc.vector.tensor_tensor(window[:].indirect(offsets[:]), esub[:], emeta[:], ALU.add)
+            nc.sync.dma_start(out[c * P : (c + 1) * P, :], window[:])

@@ -28,8 +28,7 @@ def tile_sgencoder_b_kernel(
     nc = tc.nc
     with (
         tc.tile_pool(name="held", bufs=1) as held,
-        tc.tile_pool(name="work", bufs=2) as work,
-        tc.psum_pool(name="psum", bufs=2) as psum,
+        tc.psum_pool(name="psum", bufs=4) as psum,
     ):
         offsets = held.tile([P, N // 16], U16, name="offsets")
         nc.sync.dma_start(offsets[:], offs)
@@ -51,7 +50,7 @@ def tile_sgencoder_b_kernel(
             nc.scalar.dma_start(
                 rows[v * BLOCKS : (v + 1) * BLOCKS, :], vector.rearrange("(b p) o -> b (p o)", p=P)
             )
-        cols_ps = psum.tile([P, CHUNK], F32, name="cols_ps", tag="turned", bufs=4)
+        cols_ps = psum.tile([P, CHUNK], F32, name="cols_ps", tag="bank")
         nc.tensor.transpose(cols_ps[:, 0:P], rows[:], ident[:])
         cols = held.tile([P, P], F32, name="cols")
         nc.vector.tensor_copy(cols[:], cols_ps[:, 0:P])
@@ -72,105 +71,123 @@ def tile_sgencoder_b_kernel(
         g1 = [held.tile([P, N], BF16, name=f"g1_{b}") for b in range(BLOCKS)]
         g2 = [held.tile([P, N], BF16, name=f"g2_{b}") for b in range(BLOCKS)]
 
-        def pool_nodes(q):
-            pooled = work.tile([P, 2 * BLOCKS, CHUNK], BF16, name="pooled")
-            for b in range(BLOCKS):
-                nodes_sb = work.tile([P, NODES, CHUNK], F32, name="nodes_sb", bufs=4)
-                nc.sync.dma_start(
-                    nodes_sb[:], nodes[b * P : (b + 1) * P, :, q * CHUNK : (q + 1) * CHUNK]
-                )
-                pair_sum = work.tile([P, 2, CHUNK], F32, name="pair_sum")
-                nc.gpsimd.tensor_tensor(pair_sum[:], nodes_sb[:, 0:2, :], nodes_sb[:, 2:4, :], ALU.add)
-                nc.gpsimd.tensor_tensor(pooled[:, b, :], pair_sum[:, 0, :], pair_sum[:, 1, :], ALU.add)
-                pair_max = work.tile([P, 2, CHUNK], F32, name="pair_max")
-                nc.vector.tensor_tensor(pair_max[:], nodes_sb[:, 0:2, :], nodes_sb[:, 2:4, :], ALU.max)
-                nc.vector.tensor_tensor(
-                    pooled[:, BLOCKS + b, :], pair_max[:, 0, :], pair_max[:, 1, :], ALU.max
-                )
-            return pooled
-
-        def hidden_layer(q, terms, bias_rows, gain, shift, g):
-            total = work.tile([P, SUBS], F32, name="total", bufs=4)
-            u = [work.tile([P, D], F32, name="u", bufs=2 * SUBS) for s in range(SUBS)]
-            for s in range(SUBS):
-                u_ps = psum.tile([P, D], F32, name="u_ps")
-                for i, (inputs, weights) in enumerate(terms):
-                    nc.tensor.matmul(
-                        u_ps[:],
-                        inputs[:, s * P : (s + 1) * P],
-                        weights,
-                        start=(i == 0),
-                        stop=(i == len(terms) - 1),
+        def place(c, pool):
+            results = []
+            for name, g, weights, bias in (("esub", g1, w2_sb, 4), ("emeta", g2, v2_sb, 5)):
+                result = pool.tile([P, N], F32, name=f"{name}{c}")
+                for q in range(N_CHUNKS):
+                    o_ps = psum.tile([P, CHUNK], F32, name="o_ps", tag="bank")
+                    for b in range(BLOCKS):
+                        nc.tensor.matmul(
+                            o_ps[:],
+                            weights[:, b, c * P : (c + 1) * P],
+                            g[b][:, q * CHUNK : (q + 1) * CHUNK],
+                            start=(b == 0),
+                            stop=(b == BLOCKS - 1),
+                        )
+                    nc.scalar.activation(
+                        result[:, q * CHUNK : (q + 1) * CHUNK], o_ps[:], ACT.Identity, bias=column(bias, c)
                     )
-                nc.vector.scalar_tensor_tensor(
-                    u[s][:], u_ps[:], 1.0, bias_rows[:], ALU.mult, ALU.add, accum_out=total[:, s : s + 1]
-                )
-            neg_mean = work.tile([P, SUBS], F32, name="neg_mean", bufs=4)
-            nc.vector.tensor_scalar_mul(neg_mean[:], total[:], -1.0 / D)
-
-            sq_total = work.tile([P, SUBS], F32, name="sq_total", bufs=4)
-            for s in range(SUBS):
-                squares = work.tile([P, D], BF16, name="squares")
-                nc.scalar.activation(
-                    squares[:],
-                    u[s][:],
-                    ACT.Square,
-                    bias=neg_mean[:, s : s + 1],
-                    accum_out=sq_total[:, s : s + 1],
-                )
-            var_eps = work.tile([P, SUBS], F32, name="var_eps", bufs=4)
-            nc.gpsimd.tensor_scalar(var_eps[:], sq_total[:], 1.0 / D, EPS, ALU.mult, ALU.add)
-            rstd = work.tile([P, SUBS], F32, name="rstd", bufs=4)
-            nc.gpsimd.tensor_tensor(rstd[:], var_eps[:], neg_half[:], ALU.pow)
-
-            normed = [work.tile([P, D], F32, name="normed", bufs=2 * SUBS) for s in range(SUBS)]
-            for s in range(SUBS):
-                nc.vector.tensor_scalar(
-                    normed[s][:], u[s][:], neg_mean[:, s : s + 1], rstd[:, s : s + 1], ALU.add, ALU.mult
-                )
-
-            for b in range(BLOCKS):
-                turned = psum.tile([P, CHUNK], F32, name="turned", bufs=4)
-                for s in range(SUBS):
-                    nc.tensor.transpose(
-                        turned[:, s * P : (s + 1) * P], normed[s][:, b * P : (b + 1) * P], ident[:]
-                    )
-                nc.scalar.activation(
-                    g[b][:, q * CHUNK : (q + 1) * CHUNK],
-                    turned[:],
-                    ACT.Gelu_apprx_tanh,
-                    bias=column(shift, b),
-                    scale=column(gain, b),
-                )
-
-        def output_layer(c, g, weights, bias, result):
-            for q in range(N_CHUNKS):
-                o_ps = psum.tile([P, CHUNK], F32, name="o_ps")
-                for b in range(BLOCKS):
-                    nc.tensor.matmul(
-                        o_ps[:],
-                        weights[:, b, c * P : (c + 1) * P],
-                        g[b][:, q * CHUNK : (q + 1) * CHUNK],
-                        start=(b == 0),
-                        stop=(b == BLOCKS - 1),
-                    )
-                nc.scalar.activation(
-                    result[:, q * CHUNK : (q + 1) * CHUNK], o_ps[:], ACT.Identity, bias=column(bias, c)
-                )
-
-        for q in range(N_CHUNKS):
-            pooled = pool_nodes(q)
-            hidden_layer(q, [(meta_sb[:, q * CHUNK : (q + 1) * CHUNK], v1_sb[:])], c1_rows, 2, 3, g2)
-            hidden_layer(
-                q, [(pooled[:, i, :], w1_sb[:, i, :]) for i in range(2 * BLOCKS)], b1_rows, 0, 1, g1
-            )
-
-        for c in range(BLOCKS):
-            esub = work.tile([P, N], F32, name="esub")
-            output_layer(c, g1, w2_sb, 4, esub)
-            emeta = work.tile([P, N], F32, name="emeta")
-            output_layer(c, g2, v2_sb, 5, emeta)
-            window = work.tile([P, SLOTS], F32, name="window")
+                results.append(result)
+            esub, emeta = results
+            window = pool.tile([P, SLOTS], F32, name=f"window{c}")
             nc.sync.dma_start(window[:], base[c * P : (c + 1) * P, :])
             nc.vector.tensor_tensor(window[:].indirect(offsets[:]), esub[:], emeta[:], ALU.add)
             nc.sync.dma_start(out[c * P : (c + 1) * P, :], window[:])
+
+        with tc.tile_pool(name="first", bufs=1) as first:
+            with tc.tile_pool(name="work", bufs=2) as work:
+
+                def norm_gelu(q, linear_ps, bias_rows, gain, shift, g):
+                    total = work.tile([P, SUBS], F32, name="total", bufs=4)
+                    u = [work.tile([P, D], F32, name="u", bufs=2 * SUBS) for s in range(SUBS)]
+                    for s in range(SUBS):
+                        nc.vector.scalar_tensor_tensor(
+                            u[s][:],
+                            linear_ps[s][:],
+                            1.0,
+                            bias_rows[:],
+                            ALU.mult,
+                            ALU.add,
+                            accum_out=total[:, s : s + 1],
+                        )
+                    neg_mean = work.tile([P, SUBS], F32, name="neg_mean", bufs=4)
+                    nc.vector.tensor_scalar_mul(neg_mean[:], total[:], -1.0 / D)
+
+                    sq_total = work.tile([P, SUBS], F32, name="sq_total", bufs=4)
+                    for s in range(SUBS):
+                        squares = work.tile([P, D], BF16, name="squares")
+                        nc.scalar.activation(
+                            squares[:],
+                            u[s][:],
+                            ACT.Square,
+                            bias=neg_mean[:, s : s + 1],
+                            accum_out=sq_total[:, s : s + 1],
+                        )
+                    var_eps = work.tile([P, SUBS], F32, name="var_eps", bufs=4)
+                    nc.gpsimd.tensor_scalar(var_eps[:], sq_total[:], 1.0 / D, EPS, ALU.mult, ALU.add)
+                    rstd = work.tile([P, SUBS], F32, name="rstd", bufs=4)
+                    nc.gpsimd.tensor_tensor(rstd[:], var_eps[:], neg_half[:], ALU.pow)
+                    offset = work.tile([P, SUBS], F32, name="offset", bufs=4)
+                    nc.gpsimd.tensor_tensor(offset[:], neg_mean[:], rstd[:], ALU.mult)
+
+                    normed = [work.tile([P, D], F32, name="normed", bufs=2 * SUBS) for s in range(SUBS)]
+                    for s in range(SUBS):
+                        nc.scalar.activation(
+                            normed[s][:],
+                            u[s][:],
+                            ACT.Identity,
+                            bias=offset[:, s : s + 1],
+                            scale=rstd[:, s : s + 1],
+                        )
+
+                    for b in range(BLOCKS):
+                        turned = psum.tile([P, CHUNK], F32, name="turned", tag="bank")
+                        for s in range(SUBS):
+                            nc.tensor.transpose(
+                                turned[:, s * P : (s + 1) * P], normed[s][:, b * P : (b + 1) * P], ident[:]
+                            )
+                        nc.scalar.activation(
+                            g[b][:, q * CHUNK : (q + 1) * CHUNK],
+                            turned[:],
+                            ACT.Gelu_apprx_tanh,
+                            bias=column(shift, b),
+                            scale=column(gain, b),
+                        )
+
+                for q in range(N_CHUNKS):
+                    t_ps = [psum.tile([P, D], F32, name="t_ps", tag="bank") for s in range(SUBS)]
+                    for s in range(SUBS):
+                        first_sub = (q * SUBS + s) * P
+                        nc.tensor.matmul(
+                            t_ps[s][:], meta_sb[:, first_sub : first_sub + P], v1_sb[:], start=True, stop=True
+                        )
+                    norm_gelu(q, t_ps, c1_rows, 2, 3, g2)
+
+                for q in range(N_CHUNKS):
+                    pooled = work.tile([P, 2 * BLOCKS, CHUNK], BF16, name="pooled")
+                    u_ps = [psum.tile([P, D], F32, name="u_ps") for s in range(SUBS)]
+                    for b in range(BLOCKS):
+                        nodes_sb = work.tile([P, NODES, CHUNK], F32, name="nodes_sb", bufs=6)
+                        nc.sync.dma_start(
+                            nodes_sb[:], nodes[b * P : (b + 1) * P, :, q * CHUNK : (q + 1) * CHUNK]
+                        )
+                        for row, op in ((b, ALU.add), (BLOCKS + b, ALU.max)):
+                            pair = work.tile([P, 2, CHUNK], F32, name="pair")
+                            nc.vector.tensor_tensor(pair[:], nodes_sb[:, 0:2, :], nodes_sb[:, 2:4, :], op)
+                            nc.vector.tensor_tensor(pooled[:, row, :], pair[:, 0, :], pair[:, 1, :], op)
+                        for row in (b, BLOCKS + b):
+                            for s in range(SUBS):
+                                nc.tensor.matmul(
+                                    u_ps[s][:],
+                                    pooled[:, row, s * P : (s + 1) * P],
+                                    w1_sb[:, row, :],
+                                    start=(row == 0),
+                                    stop=(row == 2 * BLOCKS - 1),
+                                )
+                    norm_gelu(q, u_ps, b1_rows, 0, 1, g1)
+
+            place(0, first)
+            with tc.tile_pool(name="rest", bufs=1) as rest:
+                for c in range(1, BLOCKS):
+                    place(c, rest)

@@ -28,7 +28,7 @@ def tile_sgencoder_b_kernel(
     nc = tc.nc
     with (
         tc.tile_pool(name="held", bufs=1) as held,
-        tc.psum_pool(name="psum", bufs=4) as psum,
+        tc.psum_pool(name="psum", bufs=2) as psum,
     ):
         offsets = held.tile([P, N // 16], U16, name="offsets")
         nc.sync.dma_start(offsets[:], offs)
@@ -39,6 +39,8 @@ def tile_sgencoder_b_kernel(
         nc.scalar.dma_start(v1_sb[:], v1)
         c1_rows = held.tile([P, D], F32, name="c1_rows")
         nc.scalar.dma_start(c1_rows[:], c1.rearrange("h o -> (h o)").partition_broadcast(P))
+        w1_sb = held.tile([P, 2 * BLOCKS, D], BF16, name="w1_sb")
+        nc.scalar.dma_start(w1_sb[:], w1.rearrange("(b p) h -> p b h", p=P))
         b1_rows = held.tile([P, D], F32, name="b1_rows")
         nc.scalar.dma_start(b1_rows[:], b1.rearrange("h o -> (h o)").partition_broadcast(P))
 
@@ -50,20 +52,16 @@ def tile_sgencoder_b_kernel(
             nc.scalar.dma_start(
                 rows[v * BLOCKS : (v + 1) * BLOCKS, :], vector.rearrange("(b p) o -> b (p o)", p=P)
             )
-        cols_ps = psum.tile([P, CHUNK], F32, name="cols_ps", tag="bank")
-        nc.tensor.transpose(cols_ps[:, 0:P], rows[:], ident[:])
+        cols_ps = psum.tile([P, BLOCKS, P], F32, name="cols_ps", tag="turned")
+        nc.tensor.transpose(cols_ps[:, 0, :], rows[:], ident[:])
         cols = held.tile([P, P], F32, name="cols")
-        nc.vector.tensor_copy(cols[:], cols_ps[:, 0:P])
+        nc.vector.tensor_copy(cols[:], cols_ps[:, 0, :])
 
         def column(v, b):
             return cols[:, v * BLOCKS + b : v * BLOCKS + b + 1]
 
-        w1_sb = held.tile([P, 2 * BLOCKS, D], BF16, name="w1_sb")
-        nc.scalar.dma_start(w1_sb[:], w1.rearrange("(b p) h -> p b h", p=P))
         w2_sb = held.tile([P, BLOCKS, D], BF16, name="w2_sb")
-        nc.scalar.dma_start(w2_sb[:], w2.rearrange("(b p) c -> p b c", p=P))
         v2_sb = held.tile([P, BLOCKS, D], BF16, name="v2_sb")
-        nc.scalar.dma_start(v2_sb[:], v2.rearrange("(b p) c -> p b c", p=P))
 
         neg_half = held.tile([P, SUBS], F32, name="neg_half")
         nc.vector.memset(neg_half[:], -0.5)
@@ -73,10 +71,10 @@ def tile_sgencoder_b_kernel(
 
         def place(c, pool):
             results = []
-            for name, g, weights, bias in (("esub", g1, w2_sb, 4), ("emeta", g2, v2_sb, 5)):
+            for name, g, weights, bias in (("emeta", g2, v2_sb, 5), ("esub", g1, w2_sb, 4)):
                 result = pool.tile([P, N], F32, name=f"{name}{c}")
                 for q in range(N_CHUNKS):
-                    o_ps = psum.tile([P, CHUNK], F32, name="o_ps", tag="bank")
+                    o_ps = psum.tile([P, CHUNK], F32, name="o_ps", tag="product")
                     for b in range(BLOCKS):
                         nc.tensor.matmul(
                             o_ps[:],
@@ -89,7 +87,7 @@ def tile_sgencoder_b_kernel(
                         result[:, q * CHUNK : (q + 1) * CHUNK], o_ps[:], ACT.Identity, bias=column(bias, c)
                     )
                 results.append(result)
-            esub, emeta = results
+            emeta, esub = results
             window = pool.tile([P, SLOTS], F32, name=f"window{c}")
             nc.sync.dma_start(window[:], base[c * P : (c + 1) * P, :])
             nc.vector.tensor_tensor(window[:].indirect(offsets[:]), esub[:], emeta[:], ALU.add)
@@ -100,63 +98,47 @@ def tile_sgencoder_b_kernel(
 
                 def norm_gelu(q, linear_ps, bias_rows, gain, shift, g):
                     total = work.tile([P, SUBS], F32, name="total", bufs=4)
-                    u = [work.tile([P, D], F32, name="u", bufs=2 * SUBS) for s in range(SUBS)]
-                    for s in range(SUBS):
-                        nc.vector.scalar_tensor_tensor(
-                            u[s][:],
-                            linear_ps[s][:],
-                            1.0,
-                            bias_rows[:],
-                            ALU.mult,
-                            ALU.add,
-                            accum_out=total[:, s : s + 1],
-                        )
                     neg_mean = work.tile([P, SUBS], F32, name="neg_mean", bufs=4)
-                    nc.vector.tensor_scalar_mul(neg_mean[:], total[:], -1.0 / D)
-
                     sq_total = work.tile([P, SUBS], F32, name="sq_total", bufs=4)
+                    u = [work.tile([P, D], F32, name="u", bufs=3 * SUBS) for s in range(SUBS)]
                     for s in range(SUBS):
+                        one = slice(s, s + 1)
+                        nc.vector.scalar_tensor_tensor(
+                            u[s][:], linear_ps[s][:], 1.0, bias_rows[:], ALU.mult, ALU.add, accum_out=total[:, one]
+                        )
+                        nc.vector.tensor_scalar_mul(neg_mean[:, one], total[:, one], -1.0 / D)
                         squares = work.tile([P, D], BF16, name="squares")
                         nc.scalar.activation(
-                            squares[:],
-                            u[s][:],
-                            ACT.Square,
-                            bias=neg_mean[:, s : s + 1],
-                            accum_out=sq_total[:, s : s + 1],
+                            squares[:], u[s][:], ACT.Square, bias=neg_mean[:, one], accum_out=sq_total[:, one]
                         )
                     var_eps = work.tile([P, SUBS], F32, name="var_eps", bufs=4)
-                    nc.gpsimd.tensor_scalar(var_eps[:], sq_total[:], 1.0 / D, EPS, ALU.mult, ALU.add)
+                    nc.vector.tensor_scalar(var_eps[:], sq_total[:], 1.0 / D, EPS, ALU.mult, ALU.add)
                     rstd = work.tile([P, SUBS], F32, name="rstd", bufs=4)
                     nc.gpsimd.tensor_tensor(rstd[:], var_eps[:], neg_half[:], ALU.pow)
                     offset = work.tile([P, SUBS], F32, name="offset", bufs=4)
-                    nc.gpsimd.tensor_tensor(offset[:], neg_mean[:], rstd[:], ALU.mult)
+                    nc.vector.tensor_tensor(offset[:], neg_mean[:], rstd[:], ALU.mult)
 
-                    normed = [work.tile([P, D], F32, name="normed", bufs=2 * SUBS) for s in range(SUBS)]
                     for s in range(SUBS):
+                        one = slice(s, s + 1)
+                        normed = work.tile([P, D], F32, name="normed", bufs=4)
                         nc.scalar.activation(
-                            normed[s][:],
-                            u[s][:],
-                            ACT.Identity,
-                            bias=offset[:, s : s + 1],
-                            scale=rstd[:, s : s + 1],
+                            normed[:], u[s][:], ACT.Identity, bias=offset[:, one], scale=rstd[:, one]
                         )
-
-                    for b in range(BLOCKS):
-                        turned = psum.tile([P, CHUNK], F32, name="turned", tag="bank")
-                        for s in range(SUBS):
-                            nc.tensor.transpose(
-                                turned[:, s * P : (s + 1) * P], normed[s][:, b * P : (b + 1) * P], ident[:]
+                        turned = psum.tile([P, BLOCKS, P], F32, name="turned")
+                        first_sub = (q * SUBS + s) * P
+                        for b in range(BLOCKS):
+                            nc.tensor.transpose(turned[:, b, :], normed[:, b * P : (b + 1) * P], ident[:])
+                        for b in range(BLOCKS):
+                            nc.scalar.activation(
+                                g[b][:, first_sub : first_sub + P],
+                                turned[:, b, :],
+                                ACT.Gelu_apprx_tanh,
+                                bias=column(shift, b),
+                                scale=column(gain, b),
                             )
-                        nc.scalar.activation(
-                            g[b][:, q * CHUNK : (q + 1) * CHUNK],
-                            turned[:],
-                            ACT.Gelu_apprx_tanh,
-                            bias=column(shift, b),
-                            scale=column(gain, b),
-                        )
 
                 for q in range(N_CHUNKS):
-                    t_ps = [psum.tile([P, D], F32, name="t_ps", tag="bank") for s in range(SUBS)]
+                    t_ps = [psum.tile([P, D], F32, name="t_ps", tag="product") for s in range(SUBS)]
                     for s in range(SUBS):
                         first_sub = (q * SUBS + s) * P
                         nc.tensor.matmul(
@@ -166,7 +148,7 @@ def tile_sgencoder_b_kernel(
 
                 for q in range(N_CHUNKS):
                     pooled = work.tile([P, 2 * BLOCKS, CHUNK], BF16, name="pooled")
-                    u_ps = [psum.tile([P, D], F32, name="u_ps") for s in range(SUBS)]
+                    u_ps = [psum.tile([P, D], F32, name="u_ps", bufs=SUBS) for s in range(SUBS)]
                     for b in range(BLOCKS):
                         nodes_sb = work.tile([P, NODES, CHUNK], F32, name="nodes_sb", bufs=6)
                         nc.sync.dma_start(
@@ -187,6 +169,8 @@ def tile_sgencoder_b_kernel(
                                 )
                     norm_gelu(q, u_ps, b1_rows, 0, 1, g1)
 
+            nc.sync.dma_start(w2_sb[:], w2.rearrange("(b p) c -> p b c", p=P))
+            nc.sync.dma_start(v2_sb[:], v2.rearrange("(b p) c -> p b c", p=P))
             place(0, first)
             with tc.tile_pool(name="rest", bufs=1) as rest:
                 for c in range(1, BLOCKS):

@@ -6,6 +6,7 @@ BF16 = mybir.dt.bfloat16
 U16 = mybir.dt.uint16
 ALU = mybir.AluOpType
 ACT = mybir.ActivationFunctionType
+AXIS = mybir.AxisListType
 
 P = 128
 D = 512
@@ -98,7 +99,6 @@ def tile_sgencoder_b_kernel(
 
                 def norm_gelu(q, linear_ps, bias_rows, gain, shift, g):
                     total = work.tile([P, SUBS], F32, name="total", bufs=4)
-                    neg_mean = work.tile([P, SUBS], F32, name="neg_mean", bufs=4)
                     sq_total = work.tile([P, SUBS], F32, name="sq_total", bufs=4)
                     u = [work.tile([P, D], F32, name="u", bufs=3 * SUBS) for s in range(SUBS)]
                     for s in range(SUBS):
@@ -106,17 +106,21 @@ def tile_sgencoder_b_kernel(
                         nc.vector.scalar_tensor_tensor(
                             u[s][:], linear_ps[s][:], 1.0, bias_rows[:], ALU.mult, ALU.add, accum_out=total[:, one]
                         )
-                        nc.vector.tensor_scalar_mul(neg_mean[:, one], total[:, one], -1.0 / D)
                         squares = work.tile([P, D], BF16, name="squares")
                         nc.scalar.activation(
-                            squares[:], u[s][:], ACT.Square, bias=neg_mean[:, one], accum_out=sq_total[:, one]
+                            squares[:],
+                            u[s][:],
+                            ACT.Square,
+                            bias=total[:, one],
+                            scale=-float(D),
+                            accum_out=sq_total[:, one],
                         )
                     var_eps = work.tile([P, SUBS], F32, name="var_eps", bufs=4)
-                    nc.vector.tensor_scalar(var_eps[:], sq_total[:], 1.0 / D, EPS, ALU.mult, ALU.add)
+                    nc.vector.tensor_scalar(var_eps[:], sq_total[:], 1.0 / D**3, EPS, ALU.mult, ALU.add)
                     rstd = work.tile([P, SUBS], F32, name="rstd", bufs=4)
                     nc.gpsimd.tensor_tensor(rstd[:], var_eps[:], neg_half[:], ALU.pow)
                     offset = work.tile([P, SUBS], F32, name="offset", bufs=4)
-                    nc.vector.tensor_tensor(offset[:], neg_mean[:], rstd[:], ALU.mult)
+                    nc.vector.scalar_tensor_tensor(offset[:], total[:], -1.0 / D, rstd[:], ALU.mult, ALU.mult)
 
                     for s in range(SUBS):
                         one = slice(s, s + 1)
@@ -154,18 +158,28 @@ def tile_sgencoder_b_kernel(
                         nc.sync.dma_start(
                             nodes_sb[:], nodes[b * P : (b + 1) * P, :, q * CHUNK : (q + 1) * CHUNK]
                         )
-                        for row, op in ((b, ALU.add), (BLOCKS + b, ALU.max)):
-                            pair = work.tile([P, 2, CHUNK], F32, name="pair")
-                            nc.vector.tensor_tensor(pair[:], nodes_sb[:, 0:2, :], nodes_sb[:, 2:4, :], op)
-                            nc.vector.tensor_tensor(pooled[:, row, :], pair[:, 0, :], pair[:, 1, :], op)
-                        for row in (b, BLOCKS + b):
+                        nodes_last = nodes_sb[:].rearrange("p k j -> p j k")
+                        with nc.allow_low_precision(reason="float32 inside, rounded once to bfloat16"):
+                            nc.vector.tensor_reduce(pooled[:, BLOCKS + b, :], nodes_last, AXIS.X, ALU.max)
+                        if b < BLOCKS - 1:
+                            pair_sum = work.tile([P, 2, CHUNK], F32, name="pair_sum")
+                            nc.gpsimd.tensor_tensor(
+                                pair_sum[:], nodes_sb[:, 0:2, :], nodes_sb[:, 2:4, :], ALU.add
+                            )
+                            nc.gpsimd.tensor_tensor(
+                                pooled[:, b, :], pair_sum[:, 0, :], pair_sum[:, 1, :], ALU.add
+                            )
+                        else:
+                            with nc.allow_low_precision(reason="float32 inside, rounded once to bfloat16"):
+                                nc.vector.tensor_reduce(pooled[:, b, :], nodes_last, AXIS.X, ALU.add)
+                        for row in (BLOCKS + b, b):
                             for s in range(SUBS):
                                 nc.tensor.matmul(
                                     u_ps[s][:],
                                     pooled[:, row, s * P : (s + 1) * P],
                                     w1_sb[:, row, :],
-                                    start=(row == 0),
-                                    stop=(row == 2 * BLOCKS - 1),
+                                    start=(row == BLOCKS),
+                                    stop=(row == BLOCKS - 1),
                                 )
                     norm_gelu(q, u_ps, b1_rows, 0, 1, g1)
 

@@ -6,7 +6,6 @@ BF16 = mybir.dt.bfloat16
 U16 = mybir.dt.uint16
 ALU = mybir.AluOpType
 ACT = mybir.ActivationFunctionType
-AXIS = mybir.AxisListType
 
 P = 128
 D = 512
@@ -158,28 +157,22 @@ def tile_sgencoder_b_kernel(
                         nc.sync.dma_start(
                             nodes_sb[:], nodes[b * P : (b + 1) * P, :, q * CHUNK : (q + 1) * CHUNK]
                         )
-                        nodes_last = nodes_sb[:].rearrange("p k j -> p j k")
-                        with nc.allow_low_precision(reason="float32 inside, rounded once to bfloat16"):
-                            nc.vector.tensor_reduce(pooled[:, BLOCKS + b, :], nodes_last, AXIS.X, ALU.max)
-                        if b < BLOCKS - 1:
-                            pair_sum = work.tile([P, 2, CHUNK], F32, name="pair_sum")
-                            nc.gpsimd.tensor_tensor(
-                                pair_sum[:], nodes_sb[:, 0:2, :], nodes_sb[:, 2:4, :], ALU.add
-                            )
-                            nc.gpsimd.tensor_tensor(
-                                pooled[:, b, :], pair_sum[:, 0, :], pair_sum[:, 1, :], ALU.add
-                            )
-                        else:
-                            with nc.allow_low_precision(reason="float32 inside, rounded once to bfloat16"):
-                                nc.vector.tensor_reduce(pooled[:, b, :], nodes_last, AXIS.X, ALU.add)
-                        for row in (BLOCKS + b, b):
+                        pair_sum = work.tile([P, 2, CHUNK], F32, name="pair_sum")
+                        nc.vector.tensor_tensor(pair_sum[:], nodes_sb[:, 0:2, :], nodes_sb[:, 2:4, :], ALU.add)
+                        nc.vector.tensor_tensor(pooled[:, b, :], pair_sum[:, 0, :], pair_sum[:, 1, :], ALU.add)
+                        pair_max = work.tile([P, 2, CHUNK], BF16, name="pair_max")
+                        nc.vector.tensor_tensor(pair_max[:], nodes_sb[:, 0:2, :], nodes_sb[:, 2:4, :], ALU.max)
+                        nc.vector.tensor_tensor(
+                            pooled[:, BLOCKS + b, :], pair_max[:, 0, :], pair_max[:, 1, :], ALU.max
+                        )
+                        for row in (b, BLOCKS + b):
                             for s in range(SUBS):
                                 nc.tensor.matmul(
                                     u_ps[s][:],
                                     pooled[:, row, s * P : (s + 1) * P],
                                     w1_sb[:, row, :],
-                                    start=(row == BLOCKS),
-                                    stop=(row == BLOCKS - 1),
+                                    start=(row == 0),
+                                    stop=(row == 2 * BLOCKS - 1),
                                 )
                     norm_gelu(q, u_ps, b1_rows, 0, 1, g1)
 

@@ -36,7 +36,7 @@ def tile_sgencoder_b_kernel(
         meta_sb = held.tile([P, N], BF16, name="meta_sb")
         nc.scalar.dma_start(meta_sb[:], meta)
         v1_sb = held.tile([P, D], BF16, name="v1_sb")
-        nc.scalar.dma_start(v1_sb[:], v1)
+        nc.sync.dma_start(v1_sb[:], v1)
         c1_rows = held.tile([P, D], F32, name="c1_rows")
         nc.scalar.dma_start(c1_rows[:], c1.rearrange("h o -> (h o)").partition_broadcast(P))
         w1_sb = held.tile([P, 2 * BLOCKS, D], BF16, name="w1_sb")
@@ -70,24 +70,25 @@ def tile_sgencoder_b_kernel(
         g2 = [held.tile([P, N], BF16, name=f"g2_{b}") for b in range(BLOCKS)]
 
         def place(c, pool):
-            results = []
-            for name, g, weights, bias in (("emeta", g2, v2_sb, 5), ("esub", g1, w2_sb, 4)):
-                result = pool.tile([P, N], F32, name=f"{name}{c}")
-                for q in range(N_CHUNKS):
-                    o_ps = psum.tile([P, CHUNK], F32, name="o_ps", tag="product")
-                    for b in range(BLOCKS):
-                        nc.tensor.matmul(
-                            o_ps[:],
-                            weights[:, b, c * P : (c + 1) * P],
-                            g[b][:, q * CHUNK : (q + 1) * CHUNK],
-                            start=(b == 0),
-                            stop=(b == BLOCKS - 1),
-                        )
-                    nc.scalar.activation(
-                        result[:, q * CHUNK : (q + 1) * CHUNK], o_ps[:], ACT.Identity, bias=column(bias, c)
+            esub = pool.tile([P, N], F32, name=f"esub{c}")
+            emeta = pool.tile([P, N], F32, name=f"emeta{c}")
+            from_nodes = (esub, g1, w2_sb, 4)
+            from_meta = (emeta, g2, v2_sb, 5)
+            last = N_CHUNKS - 1
+            jobs = [(from_nodes, q) for q in range(last)] + [(from_meta, q) for q in range(N_CHUNKS)]
+            for (result, g, weights, bias), q in jobs + [(from_nodes, last)]:
+                o_ps = psum.tile([P, CHUNK], F32, name="o_ps", tag="product")
+                for b in range(BLOCKS):
+                    nc.tensor.matmul(
+                        o_ps[:],
+                        weights[:, b, c * P : (c + 1) * P],
+                        g[b][:, q * CHUNK : (q + 1) * CHUNK],
+                        start=(b == 0),
+                        stop=(b == BLOCKS - 1),
                     )
-                results.append(result)
-            emeta, esub = results
+                nc.scalar.activation(
+                    result[:, q * CHUNK : (q + 1) * CHUNK], o_ps[:], ACT.Identity, bias=column(bias, c)
+                )
             window = pool.tile([P, SLOTS], F32, name=f"window{c}")
             nc.sync.dma_start(window[:], base[c * P : (c + 1) * P, :])
             nc.vector.tensor_tensor(window[:].indirect(offsets[:]), esub[:], emeta[:], ALU.add)

@@ -70,25 +70,24 @@ def tile_sgencoder_b_kernel(
         g2 = [held.tile([P, N], BF16, name=f"g2_{b}") for b in range(BLOCKS)]
 
         def place(c, pool):
-            esub = pool.tile([P, N], F32, name=f"esub{c}")
-            emeta = pool.tile([P, N], F32, name=f"emeta{c}")
-            from_nodes = (esub, g1, w2_sb, 4)
-            from_meta = (emeta, g2, v2_sb, 5)
-            last = N_CHUNKS - 1
-            jobs = [(from_nodes, q) for q in range(last)] + [(from_meta, q) for q in range(N_CHUNKS)]
-            for (result, g, weights, bias), q in jobs + [(from_nodes, last)]:
-                o_ps = psum.tile([P, CHUNK], F32, name="o_ps", tag="product")
-                for b in range(BLOCKS):
-                    nc.tensor.matmul(
-                        o_ps[:],
-                        weights[:, b, c * P : (c + 1) * P],
-                        g[b][:, q * CHUNK : (q + 1) * CHUNK],
-                        start=(b == 0),
-                        stop=(b == BLOCKS - 1),
+            results = []
+            for name, g, weights, bias in (("emeta", g2, v2_sb, 5), ("esub", g1, w2_sb, 4)):
+                result = pool.tile([P, N], F32, name=f"{name}{c}")
+                for q in range(N_CHUNKS):
+                    o_ps = psum.tile([P, CHUNK], F32, name="o_ps", tag="product")
+                    for b in range(BLOCKS):
+                        nc.tensor.matmul(
+                            o_ps[:],
+                            weights[:, b, c * P : (c + 1) * P],
+                            g[b][:, q * CHUNK : (q + 1) * CHUNK],
+                            start=(b == 0),
+                            stop=(b == BLOCKS - 1),
+                        )
+                    nc.scalar.activation(
+                        result[:, q * CHUNK : (q + 1) * CHUNK], o_ps[:], ACT.Identity, bias=column(bias, c)
                     )
-                nc.scalar.activation(
-                    result[:, q * CHUNK : (q + 1) * CHUNK], o_ps[:], ACT.Identity, bias=column(bias, c)
-                )
+                results.append(result)
+            emeta, esub = results
             window = pool.tile([P, SLOTS], F32, name=f"window{c}")
             nc.sync.dma_start(window[:], base[c * P : (c + 1) * P, :])
             nc.vector.tensor_tensor(window[:].indirect(offsets[:]), esub[:], emeta[:], ALU.add)
@@ -122,24 +121,23 @@ def tile_sgencoder_b_kernel(
                     offset = work.tile([P, SUBS], F32, name="offset", bufs=4)
                     nc.vector.scalar_tensor_tensor(offset[:], total[:], -1.0 / D, rstd[:], ALU.mult, ALU.mult)
 
+                    normed = [work.tile([P, D], F32, name="normed", bufs=2 * SUBS) for s in range(SUBS)]
                     for s in range(SUBS):
                         one = slice(s, s + 1)
-                        normed = work.tile([P, D], F32, name="normed", bufs=4)
                         nc.scalar.activation(
-                            normed[:], u[s][:], ACT.Identity, bias=offset[:, one], scale=rstd[:, one]
+                            normed[s][:], u[s][:], ACT.Identity, bias=offset[:, one], scale=rstd[:, one]
                         )
-                        turned = psum.tile([P, BLOCKS, P], F32, name="turned")
-                        first_sub = (q * SUBS + s) * P
-                        for b in range(BLOCKS):
-                            nc.tensor.transpose(turned[:, b, :], normed[:, b * P : (b + 1) * P], ident[:])
-                        for b in range(BLOCKS):
-                            nc.scalar.activation(
-                                g[b][:, first_sub : first_sub + P],
-                                turned[:, b, :],
-                                ACT.Gelu_apprx_tanh,
-                                bias=column(shift, b),
-                                scale=column(gain, b),
-                            )
+                    for b in range(BLOCKS):
+                        turned = psum.tile([P, SUBS, P], F32, name="turned")
+                        for s in range(SUBS):
+                            nc.tensor.transpose(turned[:, s, :], normed[s][:, b * P : (b + 1) * P], ident[:])
+                        nc.scalar.activation(
+                            g[b][:, q * CHUNK : (q + 1) * CHUNK],
+                            turned[:].rearrange("p s j -> p (s j)"),
+                            ACT.Gelu_apprx_tanh,
+                            bias=column(shift, b),
+                            scale=column(gain, b),
+                        )
 
                 for q in range(N_CHUNKS):
                     t_ps = [psum.tile([P, D], F32, name="t_ps", tag="product") for s in range(SUBS)]

@@ -41,17 +41,17 @@ def tile_sgencoder_b_kernel(
         nc.scalar.dma_start(c1_rows[:], c1.rearrange("h o -> (h o)").partition_broadcast(P))
         w1_sb = held.tile([P, 2 * BLOCKS, D], BF16, name="w1_sb")
         nc.scalar.dma_start(w1_sb[:], w1.rearrange("(b p) h -> p b h", p=P))
-        b1_rows = held.tile([P, D], F32, name="b1_rows")
-        nc.scalar.dma_start(b1_rows[:], b1.rearrange("h o -> (h o)").partition_broadcast(P))
 
         ident = held.tile([P, P], F32, name="ident")
         masks.make_identity(nc, ident[:])
         rows = held.tile([P, P], F32, name="rows")
         nc.vector.memset(rows[:], 0.0)
         for v, vector in enumerate((gain1, shift1, gain2, shift2, b2, c2)):
-            nc.scalar.dma_start(
+            nc.gpsimd.dma_start(
                 rows[v * BLOCKS : (v + 1) * BLOCKS, :], vector.rearrange("(b p) o -> b (p o)", p=P)
             )
+        b1_rows = held.tile([P, D], F32, name="b1_rows")
+        nc.gpsimd.dma_start(b1_rows[:], b1.rearrange("h o -> (h o)").partition_broadcast(P))
         cols_ps = psum.tile([P, BLOCKS, P], F32, name="cols_ps", tag="turned")
         nc.tensor.transpose(cols_ps[:, 0, :], rows[:], ident[:])
         cols = held.tile([P, P], F32, name="cols")

@@ -30,17 +30,16 @@ def tile_sgencoder_b_kernel(
         tc.tile_pool(name="held", bufs=1) as held,
         tc.psum_pool(name="psum", bufs=2) as psum,
     ):
-        offsets = held.tile([P, N // 16], U16, name="offsets")
-        nc.sync.dma_start(offsets[:], offs)
-
         meta_sb = held.tile([P, N], BF16, name="meta_sb")
-        nc.scalar.dma_start(meta_sb[:], meta)
+        nc.sync.dma_start(meta_sb[:], meta)
         v1_sb = held.tile([P, D], BF16, name="v1_sb")
         nc.sync.dma_start(v1_sb[:], v1)
         c1_rows = held.tile([P, D], F32, name="c1_rows")
-        nc.scalar.dma_start(c1_rows[:], c1.rearrange("h o -> (h o)").partition_broadcast(P))
+        nc.sync.dma_start(c1_rows[:], c1.rearrange("h o -> (h o)").partition_broadcast(P))
+        offsets = held.tile([P, N // 16], U16, name="offsets")
+        nc.sync.dma_start(offsets[:], offs)
         w1_sb = held.tile([P, 2 * BLOCKS, D], BF16, name="w1_sb")
-        nc.scalar.dma_start(w1_sb[:], w1.rearrange("(b p) h -> p b h", p=P))
+        nc.gpsimd.dma_start(w1_sb[:], w1.rearrange("(b p) h -> p b h", p=P))
 
         ident = held.tile([P, P], F32, name="ident")
         masks.make_identity(nc, ident[:])

import concourse.masks as masks
import concourse.mybir as mybir

F32 = mybir.dt.float32
BF16 = mybir.dt.bfloat16
U16 = mybir.dt.uint16
ALU = mybir.AluOpType
ACT = mybir.ActivationFunctionType

P = 128
D = 512
NODES = 4
N = 2048
SLOTS = 4096
EPS = 1e-5

CHUNK = 512
N_CHUNKS = N // CHUNK
BLOCKS = D // P
SUBS = CHUNK // P

FLOPS = 2 * N * (2 * D * D + D * D + P * D + D * D)


def tile_sgencoder_b_kernel(
    tc, nodes, meta, w1, b1, gain1, shift1, w2, b2, v1, c1, gain2, shift2, v2, c2, base, offs, out
):
    nc = tc.nc
    with (
        tc.tile_pool(name="held", bufs=1) as held,
        tc.psum_pool(name="psum", bufs=2) as psum,
    ):
        meta_sb = held.tile([P, N], BF16, name="meta_sb")
        nc.sync.dma_start(meta_sb[:], meta)
        v1_sb = held.tile([P, D], BF16, name="v1_sb")
        nc.sync.dma_start(v1_sb[:], v1)
        c1_rows = held.tile([P, D], F32, name="c1_rows")
        nc.sync.dma_start(c1_rows[:], c1.rearrange("h o -> (h o)").partition_broadcast(P))
        offsets = held.tile([P, N // 16], U16, name="offsets")
        nc.sync.dma_start(offsets[:], offs)
        w1_sb = held.tile([P, 2 * BLOCKS, D], BF16, name="w1_sb")
        nc.gpsimd.dma_start(w1_sb[:], w1.rearrange("(b p) h -> p b h", p=P))

        ident = held.tile([P, P], F32, name="ident")
        masks.make_identity(nc, ident[:])
        rows = held.tile([P, P], F32, name="rows")
        nc.vector.memset(rows[:], 0.0)
        for v, vector in enumerate((gain1, shift1, gain2, shift2, b2, c2)):
            nc.gpsimd.dma_start(
                rows[v * BLOCKS : (v + 1) * BLOCKS, :], vector.rearrange("(b p) o -> b (p o)", p=P)
            )
        b1_rows = held.tile([P, D], F32, name="b1_rows")
        nc.gpsimd.dma_start(b1_rows[:], b1.rearrange("h o -> (h o)").partition_broadcast(P))
        cols_ps = psum.tile([P, BLOCKS, P], F32, name="cols_ps", tag="turned")
        nc.tensor.transpose(cols_ps[:, 0, :], rows[:], ident[:])
        cols = held.tile([P, P], F32, name="cols")
        nc.vector.tensor_copy(cols[:], cols_ps[:, 0, :])

        def column(v, b):
            return cols[:, v * BLOCKS + b : v * BLOCKS + b + 1]

        w2_sb = held.tile([P, BLOCKS, D], BF16, name="w2_sb")
        v2_sb = held.tile([P, BLOCKS, D], BF16, name="v2_sb")

        neg_half = held.tile([P, SUBS], F32, name="neg_half")
        nc.vector.memset(neg_half[:], -0.5)

        g1 = [held.tile([P, N], BF16, name=f"g1_{b}") for b in range(BLOCKS)]
        g2 = [held.tile([P, N], BF16, name=f"g2_{b}") for b in range(BLOCKS)]

        def place(c, pool):
            results = []
            for name, g, weights, bias in (("emeta", g2, v2_sb, 5), ("esub", g1, w2_sb, 4)):
                result = pool.tile([P, N], F32, name=f"{name}{c}")
                for q in range(N_CHUNKS):
                    o_ps = psum.tile([P, CHUNK], F32, name="o_ps", tag="product")
                    for b in range(BLOCKS):
                        nc.tensor.matmul(
                            o_ps[:],
                            weights[:, b, c * P : (c + 1) * P],
                            g[b][:, q * CHUNK : (q + 1) * CHUNK],
                            start=(b == 0),
                            stop=(b == BLOCKS - 1),
                        )
                    nc.scalar.activation(
                        result[:, q * CHUNK : (q + 1) * CHUNK], o_ps[:], ACT.Identity, bias=column(bias, c)
                    )
                results.append(result)
            emeta, esub = results
            window = pool.tile([P, SLOTS], F32, name=f"window{c}")
            nc.sync.dma_start(window[:], base[c * P : (c + 1) * P, :])
            nc.vector.tensor_tensor(window[:].indirect(offsets[:]), esub[:], emeta[:], ALU.add)
            nc.sync.dma_start(out[c * P : (c + 1) * P, :], window[:])

        with tc.tile_pool(name="first", bufs=1) as first:
            with tc.tile_pool(name="work", bufs=2) as work:

                def norm_gelu(q, linear_ps, bias_rows, gain, shift, g):
                    total = work.tile([P, SUBS], F32, name="total", bufs=4)
                    sq_total = work.tile([P, SUBS], F32, name="sq_total", bufs=4)
                    u = [work.tile([P, D], F32, name="u", bufs=3 * SUBS) for s in range(SUBS)]
                    for s in range(SUBS):
                        one = slice(s, s + 1)
                        nc.vector.scalar_tensor_tensor(
                            u[s][:], linear_ps[s][:], 1.0, bias_rows[:], ALU.mult, ALU.add, accum_out=total[:, one]
                        )
                        squares = work.tile([P, D], BF16, name="squares")
                        nc.scalar.activation(
                            squares[:],
                            u[s][:],
                            ACT.Square,
                            bias=total[:, one],
                            scale=-float(D),
                            accum_out=sq_total[:, one],
                        )
                    var_eps = work.tile([P, SUBS], F32, name="var_eps", bufs=4)
                    nc.vector.tensor_scalar(var_eps[:], sq_total[:], 1.0 / D**3, EPS, ALU.mult, ALU.add)
                    rstd = work.tile([P, SUBS], F32, name="rstd", bufs=4)
                    nc.gpsimd.tensor_tensor(rstd[:], var_eps[:], neg_half[:], ALU.pow)
                    offset = work.tile([P, SUBS], F32, name="offset", bufs=4)
                    nc.vector.scalar_tensor_tensor(offset[:], total[:], -1.0 / D, rstd[:], ALU.mult, ALU.mult)

                    normed = [work.tile([P, D], F32, name="normed", bufs=2 * SUBS) for s in range(SUBS)]
                    for s in range(SUBS):
                        one = slice(s, s + 1)
                        nc.scalar.activation(
                            normed[s][:], u[s][:], ACT.Identity, bias=offset[:, one], scale=rstd[:, one]
                        )
                    for b in range(BLOCKS):
                        turned = psum.tile([P, SUBS, P], F32, name="turned")
                        for s in range(SUBS):
                            nc.tensor.transpose(turned[:, s, :], normed[s][:, b * P : (b + 1) * P], ident[:])
                        nc.scalar.activation(
                            g[b][:, q * CHUNK : (q + 1) * CHUNK],
                            turned[:].rearrange("p s j -> p (s j)"),
                            ACT.Gelu_apprx_tanh,
                            bias=column(shift, b),
                            scale=column(gain, b),
                        )

                for q in range(N_CHUNKS):
                    t_ps = [psum.tile([P, D], F32, name="t_ps", tag="product") for s in range(SUBS)]
                    for s in range(SUBS):
                        first_sub = (q * SUBS + s) * P
                        nc.tensor.matmul(
                            t_ps[s][:], meta_sb[:, first_sub : first_sub + P], v1_sb[:], start=True, stop=True
                        )
                    norm_gelu(q, t_ps, c1_rows, 2, 3, g2)

                for q in range(N_CHUNKS):
                    pooled = work.tile([P, 2 * BLOCKS, CHUNK], BF16, name="pooled")
                    u_ps = [psum.tile([P, D], F32, name="u_ps", bufs=SUBS) for s in range(SUBS)]
                    for b in range(BLOCKS):
                        nodes_sb = work.tile([P, NODES, CHUNK], F32, name="nodes_sb", bufs=6)
                        nc.sync.dma_start(
                            nodes_sb[:], nodes[b * P : (b + 1) * P, :, q * CHUNK : (q + 1) * CHUNK]
                        )
                        pair_sum = work.tile([P, 2, CHUNK], F32, name="pair_sum")
                        nc.vector.tensor_tensor(pair_sum[:], nodes_sb[:, 0:2, :], nodes_sb[:, 2:4, :], ALU.add)
                        nc.vector.tensor_tensor(pooled[:, b, :], pair_sum[:, 0, :], pair_sum[:, 1, :], ALU.add)
                        pair_max = work.tile([P, 2, CHUNK], BF16, name="pair_max")
                        nc.vector.tensor_tensor(pair_max[:], nodes_sb[:, 0:2, :], nodes_sb[:, 2:4, :], ALU.max)
                        nc.vector.tensor_tensor(
                            pooled[:, BLOCKS + b, :], pair_max[:, 0, :], pair_max[:, 1, :], ALU.max
                        )
                        for row in (b, BLOCKS + b):
                            for s in range(SUBS):
                                nc.tensor.matmul(
                                    u_ps[s][:],
                                    pooled[:, row, s * P : (s + 1) * P],
                                    w1_sb[:, row, :],
                                    start=(row == 0),
                                    stop=(row == 2 * BLOCKS - 1),
                                )
                    norm_gelu(q, u_ps, b1_rows, 0, 1, g1)

            nc.sync.dma_start(w2_sb[:], w2.rearrange("(b p) c -> p b c", p=P))
            nc.sync.dma_start(v2_sb[:], v2.rearrange("(b p) c -> p b c", p=P))
            place(0, first)
            with tc.tile_pool(name="rest", bufs=1) as rest:
                for c in range(1, BLOCKS):
                    place(c, rest)
